import numpy as np
import ml_dtypes


def mxq(x, axis, fmt="e4m3"):
    dtype, down = {"e4m3": (ml_dtypes.float8_e4m3fn, 7), "e5m2": (ml_dtypes.float8_e5m2, 14)}[fmt]
    v = np.moveaxis(np.asarray(x, np.float32).astype(ml_dtypes.bfloat16).astype(np.float64), axis, -1)
    blocks = v.reshape(v.shape[:-1] + (-1, 32))
    amax = np.abs(blocks).max(-1, keepdims=True)
    byte = np.maximum(np.where(amax > 0, np.frexp(amax)[1] - 1 + 127, 0) - down, 1)
    scale = np.exp2(byte - 127.0)
    codes = (blocks / scale).astype(np.float32).astype(dtype).astype(np.float64)
    return np.moveaxis((codes * scale).reshape(v.shape), -1, axis)


WIDE = False


def mx_kscale(k):
    if not WIDE:
        return np.ones(k)
    levels = np.array([10, -10, 5, -5, 0])
    a = np.random.permutation(np.resize(levels, k // 512 * 4)).reshape(k // 512, 4)
    idx = np.arange(k)
    return np.exp2(a[idx // 512, idx % 128 // 32])


BF16 = ml_dtypes.bfloat16


def bf(x):
    return np.asarray(x, np.float32).astype(BF16)


def f64(x):
    return np.asarray(x).astype(np.float64)


B, DIN, DOUT = 1024, 512, 512

DT = 1.0
THRESH = 0.5


def setup_inputs():
    s = mx_kscale(DIN)
    return {"input_spike": bf(np.random.random((B, DIN)) * s),
            "mem": bf(0.3 + 0.5 * np.random.standard_normal((B, DOUT))),
            "spike": bf(np.random.random((B, DOUT))),
            "W_dense": bf((np.random.uniform(-1.0, 1.0, (DOUT, DIN)) * 3.0 / np.sqrt(DIN) + 11.0 / DIN) / s[None, :]),
            "b_dense": bf(np.random.standard_normal(DOUT) * 0.5),
            "W_rec": bf(np.random.uniform(-1.0, 1.0, (DOUT, DOUT)) * 3.0 / np.sqrt(DOUT)),
            "b_rec": bf(np.random.standard_normal(DOUT) * 0.5),
            "tau_m": bf(1.5 + 0.2 * np.random.standard_normal(DOUT))}


def reference(input_spike, mem, spike, W_dense, b_dense, W_rec, b_rec, tau_m):
    sp = f64(spike)
    d_input = ((mxq(f64(input_spike), 1, "e4m3") @ mxq(f64(W_dense), 1, "e4m3").T) + f64(b_dense)
               + (mxq(sp, 1, "e4m3") @ mxq(f64(W_rec), 1, "e4m3").T) + f64(b_rec))
    alpha = np.exp(-DT / f64(tau_m))
    mem_new = f64(mem) * alpha + (1.0 - alpha) * d_input - THRESH * sp
    spike_new = np.where(mem_new - THRESH > 0, 1.0, 0.0)
    return mem_new, spike_new

@@ -1,0 +1,228 @@
+from contextlib import ExitStack
+
+import concourse.mybir as mybir
+from concourse.masks import make_identity
+
+F32 = mybir.dt.float32
+BF16 = mybir.dt.bfloat16
+U32 = mybir.dt.uint32
+U8 = mybir.dt.uint8
+FP8X4 = mybir.dt.float8_e4m3fn_x4
+ALU = mybir.AluOpType
+ACT = mybir.ActivationFunctionType
+
+P = 128
+B = 1024
+D = 512
+THRESH = 0.5
+FLOPS = 2 * 2 * B * D * D
+CHUNKS = (2, 2, 4)
+PINNED = True
+
+
+def tile_spike_rnn_lif_kernel(
+    tc, input_spike, mem, spike, W_dense, b_dense, W_rec, b_rec, tau_m, out_0, out_1
+):
+    nc = tc.nc
+    with ExitStack() as ctx:
+        keep = ctx.enter_context(tc.tile_pool(name="keep", bufs=1))
+        ps_tp = ctx.enter_context(tc.psum_pool(name="ps_tp", bufs=3))
+        ps_acc = ctx.enter_context(tc.psum_pool(name="ps_acc", bufs=3))
+        ps_ty = ctx.enter_context(tc.psum_pool(name="ps_ty", bufs=2))
+        if PINNED:
+            ctx.enter_context(tc.manual_schedule())
+
+        tau_bf = keep.tile([P, 4], BF16, name="tau_bf")
+        bd_bf = keep.tile([P, 4], BF16, name="bd_bf")
+        br_bf = keep.tile([P, 4], BF16, name="br_bf")
+        with nc.allow_non_contiguous_dma(reason="three vectors of 512, two elements a run"):
+            for dst, src in ((tau_bf, tau_m), (bd_bf, b_dense), (br_bf, b_rec)):
+                nc.scalar.dma_start(
+                    out=dst[:].rearrange("p (u e) -> p u e", e=2),
+                    in_=src.rearrange("(u p e) -> p u e", u=2, e=2),
+                )
+
+        w_sb = {}
+        for name, w in (("d", W_dense), ("r", W_rec)):
+            w_sb[name] = keep.tile([P, 4 * D], BF16, name="w_sb_%s" % name)
+            nc.sync.dma_start(
+                out=w_sb[name][:].rearrange("p (u e k) -> p u e k", u=2, e=2),
+                in_=w.rearrange("(u p e) k -> p u e k", u=2, e=2),
+            )
+        starts = []
+        b0 = 0
+        for nj in CHUNKS:
+            starts.append(b0)
+            b0 += nj * P
+        x_sb, sp_sb, mem_sb = [], [], []
+        for c, nj in enumerate(CHUNKS):
+            rows = slice(starts[c], starts[c] + nj * P)
+            for lst, src, nm in ((x_sb, input_spike, "x"), (sp_sb, spike, "sp"), (mem_sb, mem, "mem")):
+                t = keep.tile([P, nj * D], BF16, name="%s_sb_%d" % (nm, c))
+                nc.sync.dma_start(out=t[:], in_=src[rows, :].rearrange("(p j) k -> p (j k)", j=nj))
+                lst.append(t)
+
+        ident = keep.tile([P, P], F32, name="ident")
+        make_identity(nc, ident[:])
+        warm = keep.tile([P, 1], F32, name="warm")
+        warm2 = keep.tile([P, 1], F32, name="warm2")
+        nc.vector.memset(warm[:], 0.0)
+        nc.scalar.activation(out=warm2[:], in_=warm[:], func=ACT.Exp)
+
+        rtau = keep.tile([P, 4], F32, name="rtau")
+        alpha = keep.tile([P, 4], F32, name="alpha")
+        gain = keep.tile([P, 4], F32, name="gain")
+        bsum = keep.tile([P, 4], F32, name="bsum")
+        cbias = keep.tile([P, 4], F32, name="cbias")
+        nc.vector.reciprocal(out=rtau[:], in_=tau_bf[:])
+        nc.scalar.activation(out=alpha[:], in_=rtau[:], func=ACT.Exp, scale=-1.0)
+        nc.vector.tensor_tensor(out=bsum[:], in0=bd_bf[:], in1=br_bf[:], op=ALU.add)
+        nc.vector.tensor_scalar(
+            out=gain[:], in0=alpha[:], scalar1=-1.0, scalar2=1.0, op0=ALU.mult, op1=ALU.add
+        )
+        nc.vector.tensor_tensor(out=cbias[:], in0=bsum[:], in1=gain[:], op=ALU.mult)
+
+        def transpose_pair(src, pair, tag):
+            bank = ps_tp.tile([P, 512], F32, name="tp_%s" % tag, tag="tp")
+            src32 = src[:].bitcast(F32)
+            for jl in range(2):
+                for uk in range(2):
+                    w0 = (2 * pair + jl) * 256 + uk * P
+                    nc.tensor.transpose(
+                        bank[:, uk * 256 + jl * P : uk * 256 + (jl + 1) * P], src32[:, w0 : w0 + P], ident[:]
+                    )
+            return bank
+
+        def evacuate(eng, bank, grouped, pair):
+            dst = grouped[:].bitcast(F32)[:, pair * 512 : (pair + 1) * 512].rearrange("p (n u) -> p n u", u=2)
+            src = bank[:].rearrange("p (u n) -> p n u", u=2)
+            if eng == "s":
+                nc.scalar.copy(out=dst, in_=src)
+            else:
+                nc.vector.tensor_copy(out=dst, in_=src)
+
+        def mx_tiles(nm, cols):
+            grouped = keep.tile([P, cols * 4], BF16, name="g_%s" % nm, align_bytes=64)
+            codes = keep.tile([P, cols], U32, name="c_%s" % nm, align_bytes=64)
+            scales = keep.tile([P, cols], U8, name="s_%s" % nm, align_bytes=64)
+            return grouped, codes, scales
+
+        def quantise(op):
+            grouped, codes, scales = op
+            nc.vector.quantize_mx(out=codes[:].bitcast(FP8X4), scales=scales[:], in_=grouped[:])
+
+        def prepare(src, nm, npairs, engines):
+            op = mx_tiles(nm, npairs * 256)
+            banks = [transpose_pair(src, pr, "%s_%d" % (nm, pr)) for pr in range(npairs)]
+            for pr in range(npairs):
+                evacuate(engines[pr], banks[pr], op[0], pr)
+            quantise(op)
+            return op
+
+        w_op = {}
+        for name in ("d", "r"):
+            w_op[name] = prepare(w_sb[name], "w%s" % name, 2, "sv")
+
+        x_op, sp_op = {}, {}
+        z_sb, y_sb, o0_sb, o1_sb = {}, {}, {}, {}
+
+        def stage_a(c, engines):
+            nj = CHUNKS[c]
+            x_op[c] = prepare(x_sb[c], "x%d" % c, nj // 2, engines)
+            sp_op[c] = prepare(sp_sb[c], "sp%d" % c, nj // 2, engines)
+
+        def stage_m(c):
+            nj = CHUNKS[c]
+            n = nj * P
+            m32 = mem_sb[c][:].bitcast(F32)
+            if nj == 4:
+                tm = [ps_tp.tile([P, 512], F32, name="tm_%d_%d" % (c, u), tag="tp") for u in range(2)]
+                reg = [tm[u][:, 0:512] for u in range(2)]
+            else:
+                tm0 = ps_tp.tile([P, 512], F32, name="tm_%d" % c, tag="tp")
+                reg = [tm0[:, u * 256 : (u + 1) * 256] for u in range(2)]
+            for u in range(2):
+                for j in range(nj):
+                    nc.tensor.transpose(
+                        reg[u][:, j * P : (j + 1) * P], m32[:, j * 256 + u * P : j * 256 + (u + 1) * P], ident[:]
+                    )
+            accs = []
+            for ot in range(4):
+                if nj == 4:
+                    acc_t = ps_acc.tile([P, 512], F32, name="acc_%d_%d" % (c, ot), tag="acc")
+                    acc = acc_t[:, 0:512]
+                else:
+                    if ot % 2 == 0:
+                        acc_t = ps_acc.tile([P, 512], F32, name="acc_%d_%d" % (c, ot), tag="acc")
+                    acc = acc_t[:, (ot % 2) * 256 : (ot % 2 + 1) * 256]
+                accs.append(acc)
+                cols = slice(ot * P, (ot + 1) * P)
+                for first, wn, act in ((True, "d", x_op[c]), (False, "r", sp_op[c])):
+                    nc.tensor.matmul_mx(
+                        out=acc,
+                        lhsT=w_op[wn][1][:, cols].bitcast(FP8X4),
+                        lhsT_scale=w_op[wn][2][:, cols],
+                        rhs=act[1][:].bitcast(FP8X4),
+                        rhs_scale=act[2][:],
+                        start=first,
+                        stop=not first,
+                    )
+            for ot in range(4):
+                u, e = divmod(ot, 2)
+                z = keep.tile([P, n], F32, name="z_%d_%d" % (c, ot))
+                z_sb[(c, ot)] = z
+                nc.scalar.activation(
+                    out=z[:],
+                    in_=reg[u].bitcast(BF16).rearrange("p (n e) -> p n e", e=2)[:, :, e],
+                    func=ACT.Identity,
+                    bias=cbias[:, ot : ot + 1],
+                    scale=alpha[:, ot : ot + 1],
+                )
+            for ot in range(4):
+                y = keep.tile([P, n], F32, name="y_%d_%d" % (c, ot))
+                y_sb[(c, ot)] = y
+                nc.vector.scalar_tensor_tensor(
+                    out=y[:],
+                    in0=accs[ot],
+                    scalar=gain[:, ot : ot + 1],
+                    in1=z_sb[(c, ot)][:],
+                    op0=ALU.mult,
+                    op1=ALU.add,
+                )
+
+        def stage_y(c):
+            nj = CHUNKS[c]
+            rows = slice(starts[c], starts[c] + nj * P)
+            o0 = keep.tile([P, nj * D], F32, name="o0_%d" % c)
+            o1 = keep.tile([P, nj * D], F32, name="o1_%d" % c)
+            for j in range(nj):
+                ty = ps_ty.tile([P, 512], F32, name="ty_%d_%d" % (c, j), tag="ty")
+                for ot in range(4):
+                    u, e = divmod(ot, 2)
+                    nc.tensor.transpose(
+                        ty[:, e * 256 + u * P : e * 256 + (u + 1) * P], y_sb[(c, ot)][:, j * P : (j + 1) * P], ident[:]
+                    )
+                cols = slice(j * D, (j + 1) * D)
+                nc.vector.scalar_tensor_tensor(
+                    out=o0[:, cols].rearrange("p (w e) -> p w e", e=2),
+                    in0=sp_sb[c][:, cols].rearrange("p (w e) -> p w e", e=2),
+                    scalar=-THRESH,
+                    in1=ty[:].rearrange("p (e w) -> p w e", e=2),
+                    op0=ALU.mult,
+                    op1=ALU.add,
+                )
+                nc.vector.tensor_single_scalar(out=o1[:, cols], in_=o0[:, cols], scalar=THRESH, op=ALU.is_gt)
+                if j % 2 == 1:
+                    pc = slice((j - 1) * D, (j + 1) * D)
+                    for dram, sb in ((out_0, o0), (out_1, o1)):
+                        nc.sync.dma_start(
+                            out=dram[rows, :].rearrange("(p j) o -> p (j o)", j=nj)[:, pc], in_=sb[:, pc]
+                        )
+
+        nchunks = len(CHUNKS)
+        stage_a(0, "sv")
+        for c in range(nchunks):
+            stage_m(c)
+            if c + 1 < nchunks:
+                stage_a(c + 1, "ss")
+            stage_y(c)

@@ -15,9 +15,9 @@ P = 128
 B = 1024
 D = 512
 THRESH = 0.5
+BIG = 2.0 ** 64
 FLOPS = 2 * 2 * B * D * D
-CHUNKS = (2, 2, 4)
-PINNED = True
+CHUNKS = (2, 2, 2, 2)
 
 
 def tile_spike_rnn_lif_kernel(
@@ -29,8 +29,7 @@ def tile_spike_rnn_lif_kernel(
         ps_tp = ctx.enter_context(tc.psum_pool(name="ps_tp", bufs=3))
         ps_acc = ctx.enter_context(tc.psum_pool(name="ps_acc", bufs=3))
         ps_ty = ctx.enter_context(tc.psum_pool(name="ps_ty", bufs=2))
-        if PINNED:
-            ctx.enter_context(tc.manual_schedule())
+        ctx.enter_context(tc.manual_schedule())
 
         tau_bf = keep.tile([P, 4], BF16, name="tau_bf")
         bd_bf = keep.tile([P, 4], BF16, name="bd_bf")
@@ -45,28 +44,30 @@ def tile_spike_rnn_lif_kernel(
         w_sb = {}
         for name, w in (("d", W_dense), ("r", W_rec)):
             w_sb[name] = keep.tile([P, 4 * D], BF16, name="w_sb_%s" % name)
-            nc.sync.dma_start(
-                out=w_sb[name][:].rearrange("p (u e k) -> p u e k", u=2, e=2),
-                in_=w.rearrange("(u p e) k -> p u e k", u=2, e=2),
-            )
+            wv = w.rearrange("(u p e) k -> p u e k", u=2, e=2)
+            sv = w_sb[name][:].rearrange("p (u e k) -> p u e k", u=2, e=2)
+            for u in range(2):
+                nc.sync.dma_start(out=sv[:, u], in_=wv[:, u])
         starts = []
         b0 = 0
         for nj in CHUNKS:
             starts.append(b0)
             b0 += nj * P
-        x_sb, sp_sb, mem_sb = [], [], []
+        act_sb = {}
         for c, nj in enumerate(CHUNKS):
             rows = slice(starts[c], starts[c] + nj * P)
-            for lst, src, nm in ((x_sb, input_spike, "x"), (sp_sb, spike, "sp"), (mem_sb, mem, "mem")):
+            for src, nm in ((input_spike, "x"), (spike, "sp"), (mem, "m")):
                 t = keep.tile([P, nj * D], BF16, name="%s_sb_%d" % (nm, c))
                 nc.sync.dma_start(out=t[:], in_=src[rows, :].rearrange("(p j) k -> p (j k)", j=nj))
-                lst.append(t)
+                act_sb[(nm, c)] = t
 
         ident = keep.tile([P, P], F32, name="ident")
         make_identity(nc, ident[:])
         warm = keep.tile([P, 1], F32, name="warm")
         warm2 = keep.tile([P, 1], F32, name="warm2")
+        negthr = keep.tile([P, 1], F32, name="negthr")
         nc.vector.memset(warm[:], 0.0)
+        nc.vector.memset(negthr[:], -THRESH)
         nc.scalar.activation(out=warm2[:], in_=warm[:], func=ACT.Exp)
 
         rtau = keep.tile([P, 4], F32, name="rtau")
@@ -82,147 +83,266 @@ def tile_spike_rnn_lif_kernel(
         )
         nc.vector.tensor_tensor(out=cbias[:], in0=bsum[:], in1=gain[:], op=ALU.mult)
 
-        def transpose_pair(src, pair, tag):
-            bank = ps_tp.tile([P, 512], F32, name="tp_%s" % tag, tag="tp")
-            src32 = src[:].bitcast(F32)
-            for jl in range(2):
-                for uk in range(2):
-                    w0 = (2 * pair + jl) * 256 + uk * P
-                    nc.tensor.transpose(
-                        bank[:, uk * 256 + jl * P : uk * 256 + (jl + 1) * P], src32[:, w0 : w0 + P], ident[:]
-                    )
-            return bank
-
-        def evacuate(eng, bank, grouped, pair):
-            dst = grouped[:].bitcast(F32)[:, pair * 512 : (pair + 1) * 512].rearrange("p (n u) -> p n u", u=2)
-            src = bank[:].rearrange("p (u n) -> p n u", u=2)
-            if eng == "s":
-                nc.scalar.copy(out=dst, in_=src)
-            else:
-                nc.vector.tensor_copy(out=dst, in_=src)
-
         def mx_tiles(nm, cols):
             grouped = keep.tile([P, cols * 4], BF16, name="g_%s" % nm, align_bytes=64)
             codes = keep.tile([P, cols], U32, name="c_%s" % nm, align_bytes=64)
             scales = keep.tile([P, cols], U8, name="s_%s" % nm, align_bytes=64)
             return grouped, codes, scales
 
-        def quantise(op):
-            grouped, codes, scales = op
-            nc.vector.quantize_mx(out=codes[:].bitcast(FP8X4), scales=scales[:], in_=grouped[:])
-
-        def prepare(src, nm, npairs, engines):
-            op = mx_tiles(nm, npairs * 256)
-            banks = [transpose_pair(src, pr, "%s_%d" % (nm, pr)) for pr in range(npairs)]
-            for pr in range(npairs):
-                evacuate(engines[pr], banks[pr], op[0], pr)
-            quantise(op)
-            return op
-
-        w_op = {}
+        ops = {}
         for name in ("d", "r"):
-            w_op[name] = prepare(w_sb[name], "w%s" % name, 2, "sv")
+            ops[("w", name)] = mx_tiles("w%s" % name, 512)
+        for c, nj in enumerate(CHUNKS):
+            ops[("x", c)] = mx_tiles("x%d" % c, nj * P)
+            ops[("sp", c)] = mx_tiles("sp%d" % c, nj * P)
+        banks = {}
+        z_sb, y_sb, o_sb = {}, {}, {}
+        for c, nj in enumerate(CHUNKS):
+            o_sb[(c, 0)] = keep.tile([P, nj * D], F32, name="o0_%d" % c)
+            o_sb[(c, 1)] = keep.tile([P, nj * D], F32, name="o1_%d" % c)
 
-        x_op, sp_op = {}, {}
-        z_sb, y_sb, o0_sb, o1_sb = {}, {}, {}, {}
+        def transpose_group(src, blk0, nblk, tag):
+            bank = ps_tp.tile([P, 512], F32, name="tp_%s" % tag, tag="tp")
+            src32 = src[:].bitcast(F32)
+            wid = nblk * P
+            for jl in range(nblk):
+                for uk in range(2):
+                    w0 = (blk0 + jl) * 256 + uk * P
+                    nc.tensor.transpose(
+                        bank[:, uk * wid + jl * P : uk * wid + (jl + 1) * P], src32[:, w0 : w0 + P], ident[:]
+                    )
+            return bank
 
-        def stage_a(c, engines):
-            nj = CHUNKS[c]
-            x_op[c] = prepare(x_sb[c], "x%d" % c, nj // 2, engines)
-            sp_op[c] = prepare(sp_sb[c], "sp%d" % c, nj // 2, engines)
+        def evacuate(eng, bank, grouped, blk0, nblk):
+            wid = nblk * P
+            dst = grouped[:].bitcast(F32)[:, blk0 * 256 : (blk0 + nblk) * 256].rearrange("p (n u) -> p n u", u=2)
+            src = bank[:, 0 : 2 * wid].rearrange("p (u n) -> p n u", u=2)
+            if eng == "s":
+                nc.scalar.copy(out=dst, in_=src)
+            else:
+                nc.vector.tensor_copy(out=dst, in_=src)
 
-        def stage_m(c):
+        def quantise(op, c0, c1):
+            grouped, codes, scales = op
+            nc.vector.quantize_mx(
+                out=codes[:, c0:c1].bitcast(FP8X4), scales=scales[:, c0:c1], in_=grouped[:, 4 * c0 : 4 * c1]
+            )
+
+        def TW(w, bk):
+            banks[("w", w, bk)] = transpose_group(w_sb[w], 2 * bk, 2, "w%s%d" % (w, bk))
+
+        def EW(w, bk, eng):
+            evacuate(eng, banks[("w", w, bk)], ops[("w", w)][0], 2 * bk, 2)
+
+        def QW(w, bk=None):
+            if bk is None:
+                quantise(ops[("w", w)], 0, 512)
+            else:
+                quantise(ops[("w", w)], bk * 256, (bk + 1) * 256)
+
+        def groups(nj):
+            return [(0, 1)] if nj == 1 else [(g * 2, 2) for g in range(nj // 2)]
+
+        def TA(o, c):
+            for blk0, nblk in groups(CHUNKS[c]):
+                banks[(o, c, blk0)] = transpose_group(act_sb[(o, c)], blk0, nblk, "%s%d_%d" % (o, c, blk0))
+
+        def EA(o, c, engs):
+            for i, (blk0, nblk) in enumerate(groups(CHUNKS[c])):
+                evacuate(engs[i % len(engs)], banks[(o, c, blk0)], ops[(o, c)][0], blk0, nblk)
+
+        def QA(o, c):
+            quantise(ops[(o, c)], 0, CHUNKS[c] * P)
+
+        def TM(c):
             nj = CHUNKS[c]
             n = nj * P
-            m32 = mem_sb[c][:].bitcast(F32)
+            m32 = act_sb[("m", c)][:].bitcast(F32)
             if nj == 4:
                 tm = [ps_tp.tile([P, 512], F32, name="tm_%d_%d" % (c, u), tag="tp") for u in range(2)]
                 reg = [tm[u][:, 0:512] for u in range(2)]
             else:
                 tm0 = ps_tp.tile([P, 512], F32, name="tm_%d" % c, tag="tp")
-                reg = [tm0[:, u * 256 : (u + 1) * 256] for u in range(2)]
+                reg = [tm0[:, u * n : (u + 1) * n] for u in range(2)]
             for u in range(2):
                 for j in range(nj):
                     nc.tensor.transpose(
                         reg[u][:, j * P : (j + 1) * P], m32[:, j * 256 + u * P : j * 256 + (u + 1) * P], ident[:]
                     )
-            accs = []
-            for ot in range(4):
-                if nj == 4:
-                    acc_t = ps_acc.tile([P, 512], F32, name="acc_%d_%d" % (c, ot), tag="acc")
-                    acc = acc_t[:, 0:512]
-                else:
-                    if ot % 2 == 0:
-                        acc_t = ps_acc.tile([P, 512], F32, name="acc_%d_%d" % (c, ot), tag="acc")
-                    acc = acc_t[:, (ot % 2) * 256 : (ot % 2 + 1) * 256]
-                accs.append(acc)
+            banks[("m", c)] = reg
+
+        def MX(c, ots=(0, 1, 2, 3)):
+            nj = CHUNKS[c]
+            n = nj * P
+            per = 4 // nj
+            for ot in ots:
+                if ot % per == 0:
+                    banks[("acct", c)] = ps_acc.tile([P, 512], F32, name="acc_%d_%d" % (c, ot), tag="acc")
+                acc = banks[("acct", c)][:, (ot % per) * n : (ot % per + 1) * n]
+                banks[("acc", c, ot)] = acc
                 cols = slice(ot * P, (ot + 1) * P)
-                for first, wn, act in ((True, "d", x_op[c]), (False, "r", sp_op[c])):
+                for first, wn, o in ((True, "d", "x"), (False, "r", "sp")):
                     nc.tensor.matmul_mx(
                         out=acc,
-                        lhsT=w_op[wn][1][:, cols].bitcast(FP8X4),
-                        lhsT_scale=w_op[wn][2][:, cols],
-                        rhs=act[1][:].bitcast(FP8X4),
-                        rhs_scale=act[2][:],
+                        lhsT=ops[("w", wn)][1][:, cols].bitcast(FP8X4),
+                        lhsT_scale=ops[("w", wn)][2][:, cols],
+                        rhs=ops[(o, c)][1][:].bitcast(FP8X4),
+                        rhs_scale=ops[(o, c)][2][:],
                         start=first,
                         stop=not first,
                     )
-            for ot in range(4):
+
+        def Z(c, ots=(0, 1, 2, 3)):
+            n = CHUNKS[c] * P
+            for ot in ots:
                 u, e = divmod(ot, 2)
                 z = keep.tile([P, n], F32, name="z_%d_%d" % (c, ot))
                 z_sb[(c, ot)] = z
                 nc.scalar.activation(
                     out=z[:],
-                    in_=reg[u].bitcast(BF16).rearrange("p (n e) -> p n e", e=2)[:, :, e],
+                    in_=banks[("m", c)][u].bitcast(BF16).rearrange("p (n e) -> p n e", e=2)[:, :, e],
                     func=ACT.Identity,
                     bias=cbias[:, ot : ot + 1],
                     scale=alpha[:, ot : ot + 1],
                 )
-            for ot in range(4):
+
+        def DD(c, ots=(0, 1, 2, 3)):
+            n = CHUNKS[c] * P
+            for ot in ots:
                 y = keep.tile([P, n], F32, name="y_%d_%d" % (c, ot))
                 y_sb[(c, ot)] = y
                 nc.vector.scalar_tensor_tensor(
                     out=y[:],
-                    in0=accs[ot],
+                    in0=banks[("acc", c, ot)],
                     scalar=gain[:, ot : ot + 1],
                     in1=z_sb[(c, ot)][:],
                     op0=ALU.mult,
                     op1=ALU.add,
                 )
 
-        def stage_y(c):
+        def TY(c, j):
+            ty = ps_ty.tile([P, 512], F32, name="ty_%d_%d" % (c, j), tag="ty")
+            for ot in range(4):
+                u, e = divmod(ot, 2)
+                nc.tensor.transpose(
+                    ty[:, e * 256 + u * P : e * 256 + (u + 1) * P], y_sb[(c, ot)][:, j * P : (j + 1) * P], ident[:]
+                )
+            banks[("ty", c, j)] = ty
+
+        def FF(c, j):
+            cols = slice(j * D, (j + 1) * D)
+            nc.vector.scalar_tensor_tensor(
+                out=o_sb[(c, 0)][:, cols].rearrange("p (w e) -> p w e", e=2),
+                in0=act_sb[("sp", c)][:, cols].rearrange("p (w e) -> p w e", e=2),
+                scalar=-THRESH,
+                in1=banks[("ty", c, j)][:].rearrange("p (e w) -> p w e", e=2),
+                op0=ALU.mult,
+                op1=ALU.add,
+            )
+
+        def GG(c, j0, j1, eng):
+            cols = slice(j0 * D, j1 * D)
+            o0 = o_sb[(c, 0)][:, cols]
+            o1 = o_sb[(c, 1)][:, cols]
+            if eng == "v":
+                nc.vector.tensor_single_scalar(out=o1, in_=o0, scalar=THRESH, op=ALU.is_gt)
+            elif eng == "g":
+                nc.gpsimd.tensor_scalar(out=o1, in0=o0, scalar1=-THRESH, scalar2=BIG, op0=ALU.add, op1=ALU.mult)
+                nc.gpsimd.tensor_scalar(out=o1, in0=o1, scalar1=1.0, scalar2=0.0, op0=ALU.min, op1=ALU.max)
+            else:
+                nc.scalar.activation(out=o1, in_=o0, func=ACT.Sign, bias=negthr[:, 0:1], scale=1.0)
+                nc.scalar.activation(out=o1, in_=o1, func=ACT.Relu)
+
+        def ST(c, which, j0, j1):
             nj = CHUNKS[c]
             rows = slice(starts[c], starts[c] + nj * P)
-            o0 = keep.tile([P, nj * D], F32, name="o0_%d" % c)
-            o1 = keep.tile([P, nj * D], F32, name="o1_%d" % c)
-            for j in range(nj):
-                ty = ps_ty.tile([P, 512], F32, name="ty_%d_%d" % (c, j), tag="ty")
-                for ot in range(4):
-                    u, e = divmod(ot, 2)
-                    nc.tensor.transpose(
-                        ty[:, e * 256 + u * P : e * 256 + (u + 1) * P], y_sb[(c, ot)][:, j * P : (j + 1) * P], ident[:]
-                    )
-                cols = slice(j * D, (j + 1) * D)
-                nc.vector.scalar_tensor_tensor(
-                    out=o0[:, cols].rearrange("p (w e) -> p w e", e=2),
-                    in0=sp_sb[c][:, cols].rearrange("p (w e) -> p w e", e=2),
-                    scalar=-THRESH,
-                    in1=ty[:].rearrange("p (e w) -> p w e", e=2),
-                    op0=ALU.mult,
-                    op1=ALU.add,
-                )
-                nc.vector.tensor_single_scalar(out=o1[:, cols], in_=o0[:, cols], scalar=THRESH, op=ALU.is_gt)
-                if j % 2 == 1:
-                    pc = slice((j - 1) * D, (j + 1) * D)
-                    for dram, sb in ((out_0, o0), (out_1, o1)):
-                        nc.sync.dma_start(
-                            out=dram[rows, :].rearrange("(p j) o -> p (j o)", j=nj)[:, pc], in_=sb[:, pc]
-                        )
+            cols = slice(j0 * D, j1 * D)
+            dram = out_0 if which == 0 else out_1
+            nc.sync.dma_start(
+                out=dram[rows, :].rearrange("(p j) o -> p (j o)", j=nj)[:, cols], in_=o_sb[(c, which)][:, cols]
+            )
 
-        nchunks = len(CHUNKS)
-        stage_a(0, "sv")
-        for c in range(nchunks):
-            stage_m(c)
-            if c + 1 < nchunks:
-                stage_a(c + 1, "ss")
-            stage_y(c)
+        TW("d", 0)
+        TW("d", 1)
+        EW("d", 0, "s")
+        EW("d", 1, "v")
+        QW("d")
+        TW("r", 0)
+        TW("r", 1)
+        EW("r", 0, "s")
+        EW("r", 1, "v")
+        QW("r")
+        TA("x", 0)
+        EA("x", 0, "s")
+        QA("x", 0)
+        TA("sp", 0)
+        EA("sp", 0, "s")
+        QA("sp", 0)
+        TM(0)
+        Z(0)
+        TA("x", 1)
+        MX(0)
+        EA("x", 1, "s")
+        TA("sp", 1)
+        TM(1)
+        TA("x", 2)
+        EA("sp", 1, "s")
+        Z(1)
+        DD(0)
+        QA("x", 1)
+        QA("sp", 1)
+        TY(0, 0)
+        TY(0, 1)
+        FF(0, 0)
+        FF(0, 1)
+        ST(0, 0, 0, 2)
+        GG(0, 0, 2, "g")
+        MX(1)
+        EA("x", 2, "s")
+        TA("sp", 2)
+        TM(2)
+        TA("x", 3)
+        EA("sp", 2, "s")
+        Z(2)
+        DD(1)
+        QA("x", 2)
+        QA("sp", 2)
+        TY(1, 0)
+        TY(1, 1)
+        FF(1, 0)
+        FF(1, 1)
+        ST(1, 0, 0, 2)
+        GG(1, 0, 2, "g")
+        ST(0, 1, 0, 2)
+        MX(2)
+        EA("x", 3, "s")
+        TA("sp", 3)
+        TM(3)
+        EA("sp", 3, "s")
+        Z(3)
+        DD(2)
+        QA("x", 3)
+        QA("sp", 3)
+        TY(2, 0)
+        TY(2, 1)
+        FF(2, 0)
+        ST(2, 0, 0, 1)
+        FF(2, 1)
+        ST(2, 0, 1, 2)
+        ST(1, 1, 0, 2)
+        MX(3)
+        DD(3)
+        GG(2, 0, 1, "v")
+        ST(2, 1, 0, 1)
+        GG(2, 1, 2, "v")
+        ST(2, 1, 1, 2)
+        TY(3, 0)
+        TY(3, 1)
+        FF(3, 0)
+        ST(3, 0, 0, 1)
+        GG(3, 0, 1, "v")
+        ST(3, 1, 0, 1)
+        FF(3, 1)
+        ST(3, 0, 1, 2)
+        GG(3, 1, 2, "v")
+        ST(3, 1, 1, 2)

@@ -63,6 +63,11 @@ def tile_spike_rnn_lif_kernel(
 
         ident = keep.tile([P, P], F32, name="ident")
         make_identity(nc, ident[:])
+        scr = ps_ty.tile([P, 512], F32, name="scr", tag="ty")
+
+        def DP(n):
+            nc.tensor.matmul(out=scr[:, 0:n], lhsT=ident[:], rhs=ident[:, 0:n], start=True, stop=True)
+
         warm = keep.tile([P, 1], F32, name="warm")
         warm2 = keep.tile([P, 1], F32, name="warm2")
         negthr = keep.tile([P, 1], F32, name="negthr")
@@ -262,23 +267,34 @@ def tile_spike_rnn_lif_kernel(
                 out=dram[rows, :].rearrange("(p j) o -> p (j o)", j=nj)[:, cols], in_=o_sb[(c, which)][:, cols]
             )
 
+        DP(128)
+        DP(128)
+        DP(128)
+        DP(128)
         TW("d", 0)
+        DP(64)
         TW("d", 1)
+        DP(64)
         EW("d", 0, "s")
         EW("d", 1, "v")
         QW("d")
         TW("r", 0)
+        DP(64)
         TW("r", 1)
+        DP(64)
         EW("r", 0, "s")
         EW("r", 1, "v")
         QW("r")
         TA("x", 0)
+        DP(64)
         EA("x", 0, "s")
         QA("x", 0)
         TA("sp", 0)
+        DP(64)
         EA("sp", 0, "s")
         QA("sp", 0)
         TM(0)
+        DP(64)
         Z(0)
         TA("x", 1)
         MX(0)

@@ -272,35 +272,36 @@ def tile_spike_rnn_lif_kernel(
         DP(128)
         DP(128)
         TW("d", 0)
-        DP(64)
+        DP(128)
         TW("d", 1)
-        DP(64)
+        DP(128)
         EW("d", 0, "s")
         EW("d", 1, "v")
         QW("d")
         TW("r", 0)
-        DP(64)
+        DP(128)
         TW("r", 1)
-        DP(64)
+        DP(128)
         EW("r", 0, "s")
         EW("r", 1, "v")
         QW("r")
         TA("x", 0)
-        DP(64)
+        DP(128)
         EA("x", 0, "s")
         QA("x", 0)
         TA("sp", 0)
-        DP(64)
+        DP(128)
         EA("sp", 0, "s")
         QA("sp", 0)
         TM(0)
-        DP(64)
+        DP(128)
         Z(0)
         TA("x", 1)
         MX(0)
         EA("x", 1, "s")
         TA("sp", 1)
         TM(1)
+        DP(64)
         TA("x", 2)
         EA("sp", 1, "s")
         Z(1)
@@ -309,14 +310,19 @@ def tile_spike_rnn_lif_kernel(
         QA("sp", 1)
         TY(0, 0)
         TY(0, 1)
+        DP(64)
         FF(0, 0)
+        ST(0, 0, 0, 1)
+        GG(0, 0, 1, "g")
         FF(0, 1)
-        ST(0, 0, 0, 2)
-        GG(0, 0, 2, "g")
+        ST(0, 0, 1, 2)
+        ST(0, 1, 0, 1)
+        GG(0, 1, 2, "g")
         MX(1)
         EA("x", 2, "s")
         TA("sp", 2)
         TM(2)
+        DP(64)
         TA("x", 3)
         EA("sp", 2, "s")
         Z(2)
@@ -325,15 +331,20 @@ def tile_spike_rnn_lif_kernel(
         QA("sp", 2)
         TY(1, 0)
         TY(1, 1)
+        DP(64)
         FF(1, 0)
+        ST(1, 0, 0, 1)
+        GG(1, 0, 1, "g")
         FF(1, 1)
-        ST(1, 0, 0, 2)
-        GG(1, 0, 2, "g")
-        ST(0, 1, 0, 2)
+        ST(1, 0, 1, 2)
+        ST(0, 1, 1, 2)
+        ST(1, 1, 0, 1)
+        GG(1, 1, 2, "g")
         MX(2)
         EA("x", 3, "s")
         TA("sp", 3)
         TM(3)
+        DP(64)
         EA("sp", 3, "s")
         Z(3)
         DD(2)
@@ -341,11 +352,12 @@ def tile_spike_rnn_lif_kernel(
         QA("sp", 3)
         TY(2, 0)
         TY(2, 1)
+        DP(64)
         FF(2, 0)
         ST(2, 0, 0, 1)
         FF(2, 1)
         ST(2, 0, 1, 2)
-        ST(1, 1, 0, 2)
+        ST(1, 1, 1, 2)
         MX(3)
         DD(3)
         GG(2, 0, 1, "v")
@@ -354,6 +366,7 @@ def tile_spike_rnn_lif_kernel(
         ST(2, 1, 1, 2)
         TY(3, 0)
         TY(3, 1)
+        DP(64)
         FF(3, 0)
         ST(3, 0, 0, 1)
         GG(3, 0, 1, "v")

@@ -27,8 +27,9 @@ def tile_spike_rnn_lif_kernel(
     with ExitStack() as ctx:
         keep = ctx.enter_context(tc.tile_pool(name="keep", bufs=1))
         ps_tp = ctx.enter_context(tc.psum_pool(name="ps_tp", bufs=3))
-        ps_acc = ctx.enter_context(tc.psum_pool(name="ps_acc", bufs=3))
+        ps_acc = ctx.enter_context(tc.psum_pool(name="ps_acc", bufs=2))
         ps_ty = ctx.enter_context(tc.psum_pool(name="ps_ty", bufs=2))
+        ps_scr = ctx.enter_context(tc.psum_pool(name="ps_scr", bufs=1))
         ctx.enter_context(tc.manual_schedule())
 
         tau_bf = keep.tile([P, 4], BF16, name="tau_bf")
@@ -63,7 +64,7 @@ def tile_spike_rnn_lif_kernel(
 
         ident = keep.tile([P, P], F32, name="ident")
         make_identity(nc, ident[:])
-        scr = ps_ty.tile([P, 512], F32, name="scr", tag="ty")
+        scr = ps_scr.tile([P, 512], F32, name="scr")
 
         def DP(n):
             nc.tensor.matmul(out=scr[:, 0:n], lhsT=ident[:], rhs=ident[:, 0:n], start=True, stop=True)
@@ -312,12 +313,9 @@ def tile_spike_rnn_lif_kernel(
         TY(0, 1)
         DP(64)
         FF(0, 0)
-        ST(0, 0, 0, 1)
-        GG(0, 0, 1, "g")
         FF(0, 1)
-        ST(0, 0, 1, 2)
-        ST(0, 1, 0, 1)
-        GG(0, 1, 2, "g")
+        ST(0, 0, 0, 2)
+        GG(0, 0, 2, "g")
         MX(1)
         EA("x", 2, "s")
         TA("sp", 2)
@@ -333,13 +331,10 @@ def tile_spike_rnn_lif_kernel(
         TY(1, 1)
         DP(64)
         FF(1, 0)
-        ST(1, 0, 0, 1)
-        GG(1, 0, 1, "g")
         FF(1, 1)
-        ST(1, 0, 1, 2)
-        ST(0, 1, 1, 2)
-        ST(1, 1, 0, 1)
-        GG(1, 1, 2, "g")
+        ST(1, 0, 0, 2)
+        GG(1, 0, 2, "g")
+        ST(0, 1, 0, 2)
         MX(2)
         EA("x", 3, "s")
         TA("sp", 3)
@@ -357,7 +352,7 @@ def tile_spike_rnn_lif_kernel(
         ST(2, 0, 0, 1)
         FF(2, 1)
         ST(2, 0, 1, 2)
-        ST(1, 1, 1, 2)
+        ST(1, 1, 0, 2)
         MX(3)
         DD(3)
         GG(2, 0, 1, "v")

@@ -313,9 +313,9 @@ def tile_spike_rnn_lif_kernel(
         TY(0, 1)
         DP(64)
         FF(0, 0)
+        GG(0, 0, 1, "g")
         FF(0, 1)
         ST(0, 0, 0, 2)
-        GG(0, 0, 2, "g")
         MX(1)
         EA("x", 2, "s")
         TA("sp", 2)
@@ -325,16 +325,17 @@ def tile_spike_rnn_lif_kernel(
         EA("sp", 2, "s")
         Z(2)
         DD(1)
+        GG(0, 1, 2, "v")
+        ST(0, 1, 0, 2)
         QA("x", 2)
         QA("sp", 2)
         TY(1, 0)
         TY(1, 1)
         DP(64)
         FF(1, 0)
+        GG(1, 0, 1, "g")
         FF(1, 1)
         ST(1, 0, 0, 2)
-        GG(1, 0, 2, "g")
-        ST(0, 1, 0, 2)
         MX(2)
         EA("x", 3, "s")
         TA("sp", 3)
@@ -343,6 +344,8 @@ def tile_spike_rnn_lif_kernel(
         EA("sp", 3, "s")
         Z(3)
         DD(2)
+        GG(1, 1, 2, "v")
+        ST(1, 1, 0, 2)
         QA("x", 3)
         QA("sp", 3)
         TY(2, 0)
@@ -350,15 +353,13 @@ def tile_spike_rnn_lif_kernel(
         DP(64)
         FF(2, 0)
         ST(2, 0, 0, 1)
+        GG(2, 0, 1, "g")
         FF(2, 1)
         ST(2, 0, 1, 2)
-        ST(1, 1, 0, 2)
         MX(3)
         DD(3)
-        GG(2, 0, 1, "v")
-        ST(2, 1, 0, 1)
         GG(2, 1, 2, "v")
-        ST(2, 1, 1, 2)
+        ST(2, 1, 0, 2)
         TY(3, 0)
         TY(3, 1)
         DP(64)

@@ -302,7 +302,6 @@ def tile_spike_rnn_lif_kernel(
         EA("x", 1, "s")
         TA("sp", 1)
         TM(1)
-        DP(64)
         TA("x", 2)
         EA("sp", 1, "s")
         Z(1)
@@ -311,7 +310,6 @@ def tile_spike_rnn_lif_kernel(
         QA("sp", 1)
         TY(0, 0)
         TY(0, 1)
-        DP(64)
         FF(0, 0)
         GG(0, 0, 1, "g")
         FF(0, 1)
@@ -320,7 +318,6 @@ def tile_spike_rnn_lif_kernel(
         EA("x", 2, "s")
         TA("sp", 2)
         TM(2)
-        DP(64)
         TA("x", 3)
         EA("sp", 2, "s")
         Z(2)
@@ -331,7 +328,6 @@ def tile_spike_rnn_lif_kernel(
         QA("sp", 2)
         TY(1, 0)
         TY(1, 1)
-        DP(64)
         FF(1, 0)
         GG(1, 0, 1, "g")
         FF(1, 1)
@@ -340,7 +336,6 @@ def tile_spike_rnn_lif_kernel(
         EA("x", 3, "s")
         TA("sp", 3)
         TM(3)
-        DP(64)
         EA("sp", 3, "s")
         Z(3)
         DD(2)
@@ -350,7 +345,6 @@ def tile_spike_rnn_lif_kernel(
         QA("sp", 3)
         TY(2, 0)
         TY(2, 1)
-        DP(64)
         FF(2, 0)
         ST(2, 0, 0, 1)
         GG(2, 0, 1, "g")
@@ -362,7 +356,6 @@ def tile_spike_rnn_lif_kernel(
         ST(2, 1, 0, 2)
         TY(3, 0)
         TY(3, 1)
-        DP(64)
         FF(3, 0)
         ST(3, 0, 0, 1)
         GG(3, 0, 1, "v")

@@ -43,24 +43,46 @@ def tile_spike_rnn_lif_kernel(
                 )
 
         w_sb = {}
-        for name, w in (("d", W_dense), ("r", W_rec)):
+        w_dram = {"d": W_dense, "r": W_rec}
+        for name in ("d", "r"):
             w_sb[name] = keep.tile([P, 4 * D], BF16, name="w_sb_%s" % name)
-            wv = w.rearrange("(u p e) k -> p u e k", u=2, e=2)
+
+        def LW(name, u):
+            wv = w_dram[name].rearrange("(u p e) k -> p u e k", u=2, e=2)
             sv = w_sb[name][:].rearrange("p (u e k) -> p u e k", u=2, e=2)
-            for u in range(2):
-                nc.sync.dma_start(out=sv[:, u], in_=wv[:, u])
+            nc.sync.dma_start(out=sv[:, u], in_=wv[:, u])
+
         starts = []
         b0 = 0
         for nj in CHUNKS:
             starts.append(b0)
             b0 += nj * P
         act_sb = {}
-        for c, nj in enumerate(CHUNKS):
+        a_dram = {"x": input_spike, "sp": spike, "m": mem}
+
+        def LA(nm, c):
+            nj = CHUNKS[c]
             rows = slice(starts[c], starts[c] + nj * P)
-            for src, nm in ((input_spike, "x"), (spike, "sp"), (mem, "m")):
-                t = keep.tile([P, nj * D], BF16, name="%s_sb_%d" % (nm, c))
-                nc.sync.dma_start(out=t[:], in_=src[rows, :].rearrange("(p j) k -> p (j k)", j=nj))
-                act_sb[(nm, c)] = t
+            t = keep.tile([P, nj * D], BF16, name="%s_sb_%d" % (nm, c))
+            nc.sync.dma_start(out=t[:], in_=a_dram[nm][rows, :].rearrange("(p j) k -> p (j k)", j=nj))
+            act_sb[(nm, c)] = t
+
+        LA("x", 0)
+        LA("sp", 0)
+        LW("d", 0)
+        LW("r", 0)
+        LW("d", 1)
+        LW("r", 1)
+        LA("m", 0)
+        LA("x", 1)
+        LA("sp", 1)
+        LA("m", 1)
+        LA("x", 2)
+        LA("sp", 2)
+        LA("m", 2)
+        LA("x", 3)
+        LA("sp", 3)
+        LA("m", 3)
 
         ident = keep.tile([P, P], F32, name="ident")
         make_identity(nc, ident[:])
@@ -226,6 +248,21 @@ def tile_spike_rnn_lif_kernel(
                     op1=ALU.add,
                 )
 
+        def DDH(c, j):
+            n = CHUNKS[c] * P
+            cols = slice(j * P, (j + 1) * P)
+            for ot in range(4):
+                if j == 0:
+                    y_sb[(c, ot)] = keep.tile([P, n], F32, name="y_%d_%d" % (c, ot))
+                nc.vector.scalar_tensor_tensor(
+                    out=y_sb[(c, ot)][:, cols],
+                    in0=banks[("acc", c, ot)][:, cols],
+                    scalar=gain[:, ot : ot + 1],
+                    in1=z_sb[(c, ot)][:, cols],
+                    op0=ALU.mult,
+                    op1=ALU.add,
+                )
+
         def TY(c, j):
             ty = ps_ty.tile([P, 512], F32, name="ty_%d_%d" % (c, j), tag="ty")
             for ot in range(4):
@@ -272,33 +309,36 @@ def tile_spike_rnn_lif_kernel(
         DP(128)
         DP(128)
         DP(128)
-        TW("d", 0)
-        DP(128)
-        TW("d", 1)
-        DP(128)
-        EW("d", 0, "s")
-        EW("d", 1, "v")
-        QW("d")
-        TW("r", 0)
-        DP(128)
-        TW("r", 1)
-        DP(128)
-        EW("r", 0, "s")
-        EW("r", 1, "v")
-        QW("r")
         TA("x", 0)
         DP(128)
         EA("x", 0, "s")
-        QA("x", 0)
         TA("sp", 0)
         DP(128)
-        EA("sp", 0, "s")
+        EA("sp", 0, "v")
+        QA("x", 0)
         QA("sp", 0)
+        TW("d", 0)
+        DP(128)
+        EW("d", 0, "s")
+        QW("d", 0)
+        TW("r", 0)
+        DP(128)
+        EW("r", 0, "s")
+        TW("d", 1)
+        DP(128)
+        EW("d", 1, "v")
+        QW("r", 0)
+        QW("d", 1)
+        TW("r", 1)
+        DP(128)
+        EW("r", 1, "s")
+        QW("r", 1)
         TM(0)
         DP(128)
         Z(0)
+        MX(0, (0, 1))
         TA("x", 1)
-        MX(0)
+        MX(0, (2, 3))
         EA("x", 1, "s")
         TA("sp", 1)
         TM(1)
@@ -346,10 +386,9 @@ def tile_spike_rnn_lif_kernel(
         TY(2, 0)
         TY(2, 1)
         FF(2, 0)
-        ST(2, 0, 0, 1)
         GG(2, 0, 1, "g")
         FF(2, 1)
-        ST(2, 0, 1, 2)
+        ST(2, 0, 0, 2)
         MX(3)
         DD(3)
         GG(2, 1, 2, "v")

@@ -310,31 +310,30 @@ def tile_spike_rnn_lif_kernel(
         DP(128)
         DP(128)
         TA("x", 0)
-        DP(128)
         EA("x", 0, "s")
         TA("sp", 0)
+        DP(128)
         DP(128)
         EA("sp", 0, "v")
         QA("x", 0)
         QA("sp", 0)
         TW("d", 0)
-        DP(128)
         EW("d", 0, "s")
         QW("d", 0)
         TW("r", 0)
         DP(128)
+        DP(128)
         EW("r", 0, "s")
         TW("d", 1)
-        DP(128)
         EW("d", 1, "v")
         QW("r", 0)
         QW("d", 1)
         TW("r", 1)
         DP(128)
+        DP(128)
         EW("r", 1, "s")
         QW("r", 1)
         TM(0)
-        DP(128)
         Z(0)
         MX(0, (0, 1))
         TA("x", 1)

@@ -15,9 +15,14 @@ P = 128
 B = 1024
 D = 512
 THRESH = 0.5
-BIG = 2.0 ** 64
+BLOCKS = 2
+ROWS = BLOCKS * P
+GROUP = 2 * P
+CHUNKS = B // ROWS
+TILES = D // P
+WORDS = D // 2
 FLOPS = 2 * 2 * B * D * D
-CHUNKS = (2, 2, 2, 2)
+STEEP = 2.0 ** 64
 
 
 def tile_spike_rnn_lif_kernel(
@@ -32,9 +37,9 @@ def tile_spike_rnn_lif_kernel(
         ps_scr = ctx.enter_context(tc.psum_pool(name="ps_scr", bufs=1))
         ctx.enter_context(tc.manual_schedule())
 
-        tau_bf = keep.tile([P, 4], BF16, name="tau_bf")
-        bd_bf = keep.tile([P, 4], BF16, name="bd_bf")
-        br_bf = keep.tile([P, 4], BF16, name="br_bf")
+        tau_bf = keep.tile([P, TILES], BF16, name="tau_bf")
+        bd_bf = keep.tile([P, TILES], BF16, name="bd_bf")
+        br_bf = keep.tile([P, TILES], BF16, name="br_bf")
         with nc.allow_non_contiguous_dma(reason="three vectors of 512, two elements a run"):
             for dst, src in ((tau_bf, tau_m), (bd_bf, b_dense), (br_bf, b_rec)):
                 nc.scalar.dma_start(
@@ -42,67 +47,54 @@ def tile_spike_rnn_lif_kernel(
                     in_=src.rearrange("(u p e) -> p u e", u=2, e=2),
                 )
 
-        w_sb = {}
         w_dram = {"d": W_dense, "r": W_rec}
-        for name in ("d", "r"):
-            w_sb[name] = keep.tile([P, 4 * D], BF16, name="w_sb_%s" % name)
+        w_sb = {}
+        for w in ("d", "r"):
+            w_sb[w] = keep.tile([P, TILES * D], BF16, name="w_sb_%s" % w)
 
-        def LW(name, u):
-            wv = w_dram[name].rearrange("(u p e) k -> p u e k", u=2, e=2)
-            sv = w_sb[name][:].rearrange("p (u e k) -> p u e k", u=2, e=2)
-            nc.sync.dma_start(out=sv[:, u], in_=wv[:, u])
+        def load_weights(w, u):
+            nc.sync.dma_start(
+                out=w_sb[w][:].rearrange("p (u e k) -> p u e k", u=2, e=2)[:, u],
+                in_=w_dram[w].rearrange("(u p e) k -> p u e k", u=2, e=2)[:, u],
+            )
 
-        starts = []
-        b0 = 0
-        for nj in CHUNKS:
-            starts.append(b0)
-            b0 += nj * P
-        act_sb = {}
         a_dram = {"x": input_spike, "sp": spike, "m": mem}
+        a_sb = {}
 
-        def LA(nm, c):
-            nj = CHUNKS[c]
-            rows = slice(starts[c], starts[c] + nj * P)
-            t = keep.tile([P, nj * D], BF16, name="%s_sb_%d" % (nm, c))
-            nc.sync.dma_start(out=t[:], in_=a_dram[nm][rows, :].rearrange("(p j) k -> p (j k)", j=nj))
-            act_sb[(nm, c)] = t
+        def load_rows(a, c):
+            a_sb[(a, c)] = keep.tile([P, BLOCKS * D], BF16, name="%s_sb_%d" % (a, c))
+            nc.sync.dma_start(
+                out=a_sb[(a, c)][:],
+                in_=a_dram[a][c * ROWS : (c + 1) * ROWS, :].rearrange("(p j) k -> p (j k)", j=BLOCKS),
+            )
 
-        LA("x", 0)
-        LA("sp", 0)
-        LW("d", 0)
-        LW("r", 0)
-        LW("d", 1)
-        LW("r", 1)
-        LA("m", 0)
-        LA("x", 1)
-        LA("sp", 1)
-        LA("m", 1)
-        LA("x", 2)
-        LA("sp", 2)
-        LA("m", 2)
-        LA("x", 3)
-        LA("sp", 3)
-        LA("m", 3)
+        load_rows("x", 0)
+        load_rows("sp", 0)
+        for u in range(2):
+            load_weights("d", u)
+            load_weights("r", u)
+        load_rows("m", 0)
+        for c in range(1, CHUNKS):
+            for a in ("x", "sp", "m"):
+                load_rows(a, c)
 
         ident = keep.tile([P, P], F32, name="ident")
         make_identity(nc, ident[:])
-        scr = ps_scr.tile([P, 512], F32, name="scr")
+        scr = ps_scr.tile([P, D], F32, name="scr")
 
-        def DP(n):
-            nc.tensor.matmul(out=scr[:, 0:n], lhsT=ident[:], rhs=ident[:, 0:n], start=True, stop=True)
+        def keep_clock():
+            nc.tensor.matmul(out=scr[:, 0:P], lhsT=ident[:], rhs=ident[:], start=True, stop=True)
 
         warm = keep.tile([P, 1], F32, name="warm")
         warm2 = keep.tile([P, 1], F32, name="warm2")
-        negthr = keep.tile([P, 1], F32, name="negthr")
         nc.vector.memset(warm[:], 0.0)
-        nc.vector.memset(negthr[:], -THRESH)
         nc.scalar.activation(out=warm2[:], in_=warm[:], func=ACT.Exp)
 
-        rtau = keep.tile([P, 4], F32, name="rtau")
-        alpha = keep.tile([P, 4], F32, name="alpha")
-        gain = keep.tile([P, 4], F32, name="gain")
-        bsum = keep.tile([P, 4], F32, name="bsum")
-        cbias = keep.tile([P, 4], F32, name="cbias")
+        rtau = keep.tile([P, TILES], F32, name="rtau")
+        alpha = keep.tile([P, TILES], F32, name="alpha")
+        gain = keep.tile([P, TILES], F32, name="gain")
+        bsum = keep.tile([P, TILES], F32, name="bsum")
+        cbias = keep.tile([P, TILES], F32, name="cbias")
         nc.vector.reciprocal(out=rtau[:], in_=tau_bf[:])
         nc.scalar.activation(out=alpha[:], in_=rtau[:], func=ACT.Exp, scale=-1.0)
         nc.vector.tensor_tensor(out=bsum[:], in0=bd_bf[:], in1=br_bf[:], op=ALU.add)
@@ -111,294 +103,227 @@ def tile_spike_rnn_lif_kernel(
         )
         nc.vector.tensor_tensor(out=cbias[:], in0=bsum[:], in1=gain[:], op=ALU.mult)
 
-        def mx_tiles(nm, cols):
-            grouped = keep.tile([P, cols * 4], BF16, name="g_%s" % nm, align_bytes=64)
-            codes = keep.tile([P, cols], U32, name="c_%s" % nm, align_bytes=64)
-            scales = keep.tile([P, cols], U8, name="s_%s" % nm, align_bytes=64)
+        def mx_operand(name, cols):
+            grouped = keep.tile([P, cols * 4], BF16, name="g_%s" % name, align_bytes=64)
+            codes = keep.tile([P, cols], U32, name="c_%s" % name, align_bytes=64)
+            scales = keep.tile([P, cols], U8, name="s_%s" % name, align_bytes=64)
             return grouped, codes, scales
 
-        ops = {}
-        for name in ("d", "r"):
-            ops[("w", name)] = mx_tiles("w%s" % name, 512)
-        for c, nj in enumerate(CHUNKS):
-            ops[("x", c)] = mx_tiles("x%d" % c, nj * P)
-            ops[("sp", c)] = mx_tiles("sp%d" % c, nj * P)
-        banks = {}
-        z_sb, y_sb, o_sb = {}, {}, {}
-        for c, nj in enumerate(CHUNKS):
-            o_sb[(c, 0)] = keep.tile([P, nj * D], F32, name="o0_%d" % c)
-            o_sb[(c, 1)] = keep.tile([P, nj * D], F32, name="o1_%d" % c)
+        w_mx = {}
+        for w in ("d", "r"):
+            w_mx[w] = mx_operand("w%s" % w, D)
+        a_mx = {}
+        for c in range(CHUNKS):
+            for a in ("x", "sp"):
+                a_mx[(a, c)] = mx_operand("%s%d" % (a, c), ROWS)
+        o_sb = {}
+        for c in range(CHUNKS):
+            for which in range(2):
+                o_sb[(c, which)] = keep.tile([P, BLOCKS * D], F32, name="o%d_%d" % (which, c))
+        bank = {}
+        z_sb = {}
+        y_sb = {}
 
-        def transpose_group(src, blk0, nblk, tag):
-            bank = ps_tp.tile([P, 512], F32, name="tp_%s" % tag, tag="tp")
-            src32 = src[:].bitcast(F32)
-            wid = nblk * P
-            for jl in range(nblk):
-                for uk in range(2):
-                    w0 = (blk0 + jl) * 256 + uk * P
+        def transpose_words(src, first, name):
+            t = ps_tp.tile([P, D], F32, name=name, tag="tp")
+            words = src[:].bitcast(F32)
+            for b in range(2):
+                for h in range(2):
                     nc.tensor.transpose(
-                        bank[:, uk * wid + jl * P : uk * wid + (jl + 1) * P], src32[:, w0 : w0 + P], ident[:]
+                        t[:, h * GROUP + b * P : h * GROUP + (b + 1) * P],
+                        words[:, (first + b) * WORDS + h * P : (first + b) * WORDS + (h + 1) * P],
+                        ident[:],
                     )
-            return bank
+            return t
 
-        def evacuate(eng, bank, grouped, blk0, nblk):
-            wid = nblk * P
-            dst = grouped[:].bitcast(F32)[:, blk0 * 256 : (blk0 + nblk) * 256].rearrange("p (n u) -> p n u", u=2)
-            src = bank[:, 0 : 2 * wid].rearrange("p (u n) -> p n u", u=2)
-            if eng == "s":
+        def copy_words(engine, t, grouped, first):
+            dst = grouped[:].bitcast(F32)[:, first * WORDS : (first + 2) * WORDS].rearrange("p (n h) -> p n h", h=2)
+            src = t[:, 0 : 2 * GROUP].rearrange("p (h n) -> p n h", h=2)
+            if engine == "scalar":
                 nc.scalar.copy(out=dst, in_=src)
             else:
                 nc.vector.tensor_copy(out=dst, in_=src)
 
-        def quantise(op, c0, c1):
-            grouped, codes, scales = op
+        def quantise(operand, c0, c1):
+            grouped, codes, scales = operand
             nc.vector.quantize_mx(
                 out=codes[:, c0:c1].bitcast(FP8X4), scales=scales[:, c0:c1], in_=grouped[:, 4 * c0 : 4 * c1]
             )
 
-        def TW(w, bk):
-            banks[("w", w, bk)] = transpose_group(w_sb[w], 2 * bk, 2, "w%s%d" % (w, bk))
+        def transpose_weights(w, u):
+            bank[(w, u)] = transpose_words(w_sb[w], 2 * u, "tp_w%s%d" % (w, u))
 
-        def EW(w, bk, eng):
-            evacuate(eng, banks[("w", w, bk)], ops[("w", w)][0], 2 * bk, 2)
+        def copy_weights(w, u, engine):
+            copy_words(engine, bank[(w, u)], w_mx[w][0], 2 * u)
 
-        def QW(w, bk=None):
-            if bk is None:
-                quantise(ops[("w", w)], 0, 512)
-            else:
-                quantise(ops[("w", w)], bk * 256, (bk + 1) * 256)
+        def quantise_weights(w, u):
+            quantise(w_mx[w], u * GROUP, (u + 1) * GROUP)
 
-        def groups(nj):
-            return [(0, 1)] if nj == 1 else [(g * 2, 2) for g in range(nj // 2)]
+        def transpose_rows(a, c):
+            bank[(a, c)] = transpose_words(a_sb[(a, c)], 0, "tp_%s%d_0" % (a, c))
 
-        def TA(o, c):
-            for blk0, nblk in groups(CHUNKS[c]):
-                banks[(o, c, blk0)] = transpose_group(act_sb[(o, c)], blk0, nblk, "%s%d_%d" % (o, c, blk0))
+        def copy_rows(a, c, engine):
+            copy_words(engine, bank[(a, c)], a_mx[(a, c)][0], 0)
 
-        def EA(o, c, engs):
-            for i, (blk0, nblk) in enumerate(groups(CHUNKS[c])):
-                evacuate(engs[i % len(engs)], banks[(o, c, blk0)], ops[(o, c)][0], blk0, nblk)
+        def quantise_rows(a, c):
+            quantise(a_mx[(a, c)], 0, ROWS)
 
-        def QA(o, c):
-            quantise(ops[(o, c)], 0, CHUNKS[c] * P)
-
-        def TM(c):
-            nj = CHUNKS[c]
-            n = nj * P
-            m32 = act_sb[("m", c)][:].bitcast(F32)
-            if nj == 4:
-                tm = [ps_tp.tile([P, 512], F32, name="tm_%d_%d" % (c, u), tag="tp") for u in range(2)]
-                reg = [tm[u][:, 0:512] for u in range(2)]
-            else:
-                tm0 = ps_tp.tile([P, 512], F32, name="tm_%d" % c, tag="tp")
-                reg = [tm0[:, u * n : (u + 1) * n] for u in range(2)]
+        def transpose_mem(c):
+            t = ps_tp.tile([P, D], F32, name="tm_%d" % c, tag="tp")
+            words = a_sb[("m", c)][:].bitcast(F32)
             for u in range(2):
-                for j in range(nj):
+                for j in range(BLOCKS):
                     nc.tensor.transpose(
-                        reg[u][:, j * P : (j + 1) * P], m32[:, j * 256 + u * P : j * 256 + (u + 1) * P], ident[:]
+                        t[:, u * ROWS + j * P : u * ROWS + (j + 1) * P],
+                        words[:, j * WORDS + u * P : j * WORDS + (u + 1) * P],
+                        ident[:],
                     )
-            banks[("m", c)] = reg
+            bank[("m", c)] = t
 
-        def MX(c, ots=(0, 1, 2, 3)):
-            nj = CHUNKS[c]
-            n = nj * P
-            per = 4 // nj
-            for ot in ots:
-                if ot % per == 0:
-                    banks[("acct", c)] = ps_acc.tile([P, 512], F32, name="acc_%d_%d" % (c, ot), tag="acc")
-                acc = banks[("acct", c)][:, (ot % per) * n : (ot % per + 1) * n]
-                banks[("acc", c, ot)] = acc
-                cols = slice(ot * P, (ot + 1) * P)
-                for first, wn, o in ((True, "d", "x"), (False, "r", "sp")):
+        def decay_mem(c):
+            for t in range(TILES):
+                u, e = divmod(t, 2)
+                z_sb[(c, t)] = keep.tile([P, ROWS], F32, name="z_%d_%d" % (c, t))
+                nc.scalar.activation(
+                    out=z_sb[(c, t)][:],
+                    in_=bank[("m", c)][:, u * ROWS : (u + 1) * ROWS]
+                    .bitcast(BF16)
+                    .rearrange("p (n e) -> p n e", e=2)[:, :, e],
+                    func=ACT.Identity,
+                    bias=cbias[:, t : t + 1],
+                    scale=alpha[:, t : t + 1],
+                )
+
+        def matmuls(c, tiles):
+            for t in tiles:
+                if t % 2 == 0:
+                    bank[("pair", c)] = ps_acc.tile([P, D], F32, name="acc_%d_%d" % (c, t), tag="acc")
+                acc = bank[("pair", c)][:, (t % 2) * ROWS : (t % 2 + 1) * ROWS]
+                bank[("acc", c, t)] = acc
+                cols = slice(t * P, (t + 1) * P)
+                for first, w, a in ((True, "d", "x"), (False, "r", "sp")):
                     nc.tensor.matmul_mx(
                         out=acc,
-                        lhsT=ops[("w", wn)][1][:, cols].bitcast(FP8X4),
-                        lhsT_scale=ops[("w", wn)][2][:, cols],
-                        rhs=ops[(o, c)][1][:].bitcast(FP8X4),
-                        rhs_scale=ops[(o, c)][2][:],
+                        lhsT=w_mx[w][1][:, cols].bitcast(FP8X4),
+                        lhsT_scale=w_mx[w][2][:, cols],
+                        rhs=a_mx[(a, c)][1][:].bitcast(FP8X4),
+                        rhs_scale=a_mx[(a, c)][2][:],
                         start=first,
                         stop=not first,
                     )
 
-        def Z(c, ots=(0, 1, 2, 3)):
-            n = CHUNKS[c] * P
-            for ot in ots:
-                u, e = divmod(ot, 2)
-                z = keep.tile([P, n], F32, name="z_%d_%d" % (c, ot))
-                z_sb[(c, ot)] = z
-                nc.scalar.activation(
-                    out=z[:],
-                    in_=banks[("m", c)][u].bitcast(BF16).rearrange("p (n e) -> p n e", e=2)[:, :, e],
-                    func=ACT.Identity,
-                    bias=cbias[:, ot : ot + 1],
-                    scale=alpha[:, ot : ot + 1],
-                )
-
-        def DD(c, ots=(0, 1, 2, 3)):
-            n = CHUNKS[c] * P
-            for ot in ots:
-                y = keep.tile([P, n], F32, name="y_%d_%d" % (c, ot))
-                y_sb[(c, ot)] = y
+        def update(c):
+            for t in range(TILES):
+                y_sb[(c, t)] = keep.tile([P, ROWS], F32, name="y_%d_%d" % (c, t))
                 nc.vector.scalar_tensor_tensor(
-                    out=y[:],
-                    in0=banks[("acc", c, ot)],
-                    scalar=gain[:, ot : ot + 1],
-                    in1=z_sb[(c, ot)][:],
+                    out=y_sb[(c, t)][:],
+                    in0=bank[("acc", c, t)],
+                    scalar=gain[:, t : t + 1],
+                    in1=z_sb[(c, t)][:],
                     op0=ALU.mult,
                     op1=ALU.add,
                 )
 
-        def DDH(c, j):
-            n = CHUNKS[c] * P
-            cols = slice(j * P, (j + 1) * P)
-            for ot in range(4):
-                if j == 0:
-                    y_sb[(c, ot)] = keep.tile([P, n], F32, name="y_%d_%d" % (c, ot))
-                nc.vector.scalar_tensor_tensor(
-                    out=y_sb[(c, ot)][:, cols],
-                    in0=banks[("acc", c, ot)][:, cols],
-                    scalar=gain[:, ot : ot + 1],
-                    in1=z_sb[(c, ot)][:, cols],
-                    op0=ALU.mult,
-                    op1=ALU.add,
-                )
-
-        def TY(c, j):
-            ty = ps_ty.tile([P, 512], F32, name="ty_%d_%d" % (c, j), tag="ty")
-            for ot in range(4):
-                u, e = divmod(ot, 2)
+        def transpose_back(c, j):
+            ty = ps_ty.tile([P, D], F32, name="ty_%d_%d" % (c, j), tag="ty")
+            for t in range(TILES):
+                u, e = divmod(t, 2)
                 nc.tensor.transpose(
-                    ty[:, e * 256 + u * P : e * 256 + (u + 1) * P], y_sb[(c, ot)][:, j * P : (j + 1) * P], ident[:]
+                    ty[:, e * WORDS + u * P : e * WORDS + (u + 1) * P], y_sb[(c, t)][:, j * P : (j + 1) * P], ident[:]
                 )
-            banks[("ty", c, j)] = ty
+            bank[("ty", c, j)] = ty
 
-        def FF(c, j):
+        def reset(c, j):
             cols = slice(j * D, (j + 1) * D)
             nc.vector.scalar_tensor_tensor(
                 out=o_sb[(c, 0)][:, cols].rearrange("p (w e) -> p w e", e=2),
-                in0=act_sb[("sp", c)][:, cols].rearrange("p (w e) -> p w e", e=2),
+                in0=a_sb[("sp", c)][:, cols].rearrange("p (w e) -> p w e", e=2),
                 scalar=-THRESH,
-                in1=banks[("ty", c, j)][:].rearrange("p (e w) -> p w e", e=2),
+                in1=bank[("ty", c, j)][:].rearrange("p (e w) -> p w e", e=2),
                 op0=ALU.mult,
                 op1=ALU.add,
             )
 
-        def GG(c, j0, j1, eng):
-            cols = slice(j0 * D, j1 * D)
-            o0 = o_sb[(c, 0)][:, cols]
-            o1 = o_sb[(c, 1)][:, cols]
-            if eng == "v":
-                nc.vector.tensor_single_scalar(out=o1, in_=o0, scalar=THRESH, op=ALU.is_gt)
-            elif eng == "g":
-                nc.gpsimd.tensor_scalar(out=o1, in0=o0, scalar1=-THRESH, scalar2=BIG, op0=ALU.add, op1=ALU.mult)
-                nc.gpsimd.tensor_scalar(out=o1, in0=o1, scalar1=1.0, scalar2=0.0, op0=ALU.min, op1=ALU.max)
+        def fire(c, j, engine):
+            cols = slice(j * D, (j + 1) * D)
+            v = o_sb[(c, 0)][:, cols]
+            s = o_sb[(c, 1)][:, cols]
+            if engine == "vector":
+                nc.vector.tensor_single_scalar(out=s, in_=v, scalar=THRESH, op=ALU.is_gt)
             else:
-                nc.scalar.activation(out=o1, in_=o0, func=ACT.Sign, bias=negthr[:, 0:1], scale=1.0)
-                nc.scalar.activation(out=o1, in_=o1, func=ACT.Relu)
+                nc.gpsimd.tensor_scalar(out=s, in0=v, scalar1=-THRESH, scalar2=STEEP, op0=ALU.add, op1=ALU.mult)
+                nc.gpsimd.tensor_scalar(out=s, in0=s, scalar1=1.0, scalar2=0.0, op0=ALU.min, op1=ALU.max)
 
-        def ST(c, which, j0, j1):
-            nj = CHUNKS[c]
-            rows = slice(starts[c], starts[c] + nj * P)
+        def store(c, which, j0, j1):
             cols = slice(j0 * D, j1 * D)
             dram = out_0 if which == 0 else out_1
             nc.sync.dma_start(
-                out=dram[rows, :].rearrange("(p j) o -> p (j o)", j=nj)[:, cols], in_=o_sb[(c, which)][:, cols]
+                out=dram[c * ROWS : (c + 1) * ROWS, :].rearrange("(p j) o -> p (j o)", j=BLOCKS)[:, cols],
+                in_=o_sb[(c, which)][:, cols],
             )
 
-        DP(128)
-        DP(128)
-        DP(128)
-        DP(128)
-        TA("x", 0)
-        EA("x", 0, "s")
-        TA("sp", 0)
-        DP(128)
-        DP(128)
-        EA("sp", 0, "v")
-        QA("x", 0)
-        QA("sp", 0)
-        TW("d", 0)
-        EW("d", 0, "s")
-        QW("d", 0)
-        TW("r", 0)
-        DP(128)
-        DP(128)
-        EW("r", 0, "s")
-        TW("d", 1)
-        EW("d", 1, "v")
-        QW("r", 0)
-        QW("d", 1)
-        TW("r", 1)
-        DP(128)
-        DP(128)
-        EW("r", 1, "s")
-        QW("r", 1)
-        TM(0)
-        Z(0)
-        MX(0, (0, 1))
-        TA("x", 1)
-        MX(0, (2, 3))
-        EA("x", 1, "s")
-        TA("sp", 1)
-        TM(1)
-        TA("x", 2)
-        EA("sp", 1, "s")
-        Z(1)
-        DD(0)
-        QA("x", 1)
-        QA("sp", 1)
-        TY(0, 0)
-        TY(0, 1)
-        FF(0, 0)
-        GG(0, 0, 1, "g")
-        FF(0, 1)
-        ST(0, 0, 0, 2)
-        MX(1)
-        EA("x", 2, "s")
-        TA("sp", 2)
-        TM(2)
-        TA("x", 3)
-        EA("sp", 2, "s")
-        Z(2)
-        DD(1)
-        GG(0, 1, 2, "v")
-        ST(0, 1, 0, 2)
-        QA("x", 2)
-        QA("sp", 2)
-        TY(1, 0)
-        TY(1, 1)
-        FF(1, 0)
-        GG(1, 0, 1, "g")
-        FF(1, 1)
-        ST(1, 0, 0, 2)
-        MX(2)
-        EA("x", 3, "s")
-        TA("sp", 3)
-        TM(3)
-        EA("sp", 3, "s")
-        Z(3)
-        DD(2)
-        GG(1, 1, 2, "v")
-        ST(1, 1, 0, 2)
-        QA("x", 3)
-        QA("sp", 3)
-        TY(2, 0)
-        TY(2, 1)
-        FF(2, 0)
-        GG(2, 0, 1, "g")
-        FF(2, 1)
-        ST(2, 0, 0, 2)
-        MX(3)
-        DD(3)
-        GG(2, 1, 2, "v")
-        ST(2, 1, 0, 2)
-        TY(3, 0)
-        TY(3, 1)
-        FF(3, 0)
-        ST(3, 0, 0, 1)
-        GG(3, 0, 1, "v")
-        ST(3, 1, 0, 1)
-        FF(3, 1)
-        ST(3, 0, 1, 2)
-        GG(3, 1, 2, "v")
-        ST(3, 1, 1, 2)
+        for keeper in range(4):
+            keep_clock()
+        transpose_rows("x", 0)
+        copy_rows("x", 0, "scalar")
+        transpose_rows("sp", 0)
+        keep_clock()
+        keep_clock()
+        copy_rows("sp", 0, "vector")
+        quantise_rows("x", 0)
+        quantise_rows("sp", 0)
+        transpose_weights("d", 0)
+        copy_weights("d", 0, "scalar")
+        quantise_weights("d", 0)
+        transpose_weights("r", 0)
+        keep_clock()
+        keep_clock()
+        copy_weights("r", 0, "scalar")
+        transpose_weights("d", 1)
+        copy_weights("d", 1, "vector")
+        quantise_weights("r", 0)
+        quantise_weights("d", 1)
+        transpose_weights("r", 1)
+        keep_clock()
+        keep_clock()
+        copy_weights("r", 1, "scalar")
+        quantise_weights("r", 1)
+        transpose_mem(0)
+        decay_mem(0)
+        matmuls(0, (0, 1))
+        transpose_rows("x", 1)
+        matmuls(0, (2, 3))
+
+        for c in range(CHUNKS):
+            if c > 0:
+                matmuls(c, (0, 1, 2, 3))
+            if c + 1 < CHUNKS:
+                copy_rows("x", c + 1, "scalar")
+                transpose_rows("sp", c + 1)
+                transpose_mem(c + 1)
+            if c + 2 < CHUNKS:
+                transpose_rows("x", c + 2)
+            if c + 1 < CHUNKS:
+                copy_rows("sp", c + 1, "scalar")
+                decay_mem(c + 1)
+            update(c)
+            if c > 0:
+                fire(c - 1, 1, "vector")
+                store(c - 1, 1, 0, BLOCKS)
+            if c + 1 < CHUNKS:
+                quantise_rows("x", c + 1)
+                quantise_rows("sp", c + 1)
+            for j in range(BLOCKS):
+                transpose_back(c, j)
+            if c + 1 < CHUNKS:
+                reset(c, 0)
+                fire(c, 0, "gpsimd")
+                reset(c, 1)
+                store(c, 0, 0, BLOCKS)
+
+        last = CHUNKS - 1
+        for j in range(BLOCKS):
+            reset(last, j)
+            store(last, 0, j, j + 1)
+            fire(last, j, "vector")
+            store(last, 1, j, j + 1)

from contextlib import ExitStack

import concourse.mybir as mybir
from concourse.masks import make_identity

F32 = mybir.dt.float32
BF16 = mybir.dt.bfloat16
U32 = mybir.dt.uint32
U8 = mybir.dt.uint8
FP8X4 = mybir.dt.float8_e4m3fn_x4
ALU = mybir.AluOpType
ACT = mybir.ActivationFunctionType

P = 128
B = 1024
D = 512
THRESH = 0.5
BLOCKS = 2
ROWS = BLOCKS * P
GROUP = 2 * P
CHUNKS = B // ROWS
TILES = D // P
WORDS = D // 2
FLOPS = 2 * 2 * B * D * D
STEEP = 2.0 ** 64


def tile_spike_rnn_lif_kernel(
    tc, input_spike, mem, spike, W_dense, b_dense, W_rec, b_rec, tau_m, out_0, out_1
):
    nc = tc.nc
    with ExitStack() as ctx:
        keep = ctx.enter_context(tc.tile_pool(name="keep", bufs=1))
        ps_tp = ctx.enter_context(tc.psum_pool(name="ps_tp", bufs=3))
        ps_acc = ctx.enter_context(tc.psum_pool(name="ps_acc", bufs=2))
        ps_ty = ctx.enter_context(tc.psum_pool(name="ps_ty", bufs=2))
        ps_scr = ctx.enter_context(tc.psum_pool(name="ps_scr", bufs=1))
        ctx.enter_context(tc.manual_schedule())

        tau_bf = keep.tile([P, TILES], BF16, name="tau_bf")
        bd_bf = keep.tile([P, TILES], BF16, name="bd_bf")
        br_bf = keep.tile([P, TILES], BF16, name="br_bf")
        with nc.allow_non_contiguous_dma(reason="three vectors of 512, two elements a run"):
            for dst, src in ((tau_bf, tau_m), (bd_bf, b_dense), (br_bf, b_rec)):
                nc.scalar.dma_start(
                    out=dst[:].rearrange("p (u e) -> p u e", e=2),
                    in_=src.rearrange("(u p e) -> p u e", u=2, e=2),
                )

        w_dram = {"d": W_dense, "r": W_rec}
        w_sb = {}
        for w in ("d", "r"):
            w_sb[w] = keep.tile([P, TILES * D], BF16, name="w_sb_%s" % w)

        def load_weights(w, u):
            nc.sync.dma_start(
                out=w_sb[w][:].rearrange("p (u e k) -> p u e k", u=2, e=2)[:, u],
                in_=w_dram[w].rearrange("(u p e) k -> p u e k", u=2, e=2)[:, u],
            )

        a_dram = {"x": input_spike, "sp": spike, "m": mem}
        a_sb = {}

        def load_rows(a, c):
            a_sb[(a, c)] = keep.tile([P, BLOCKS * D], BF16, name="%s_sb_%d" % (a, c))
            nc.sync.dma_start(
                out=a_sb[(a, c)][:],
                in_=a_dram[a][c * ROWS : (c + 1) * ROWS, :].rearrange("(p j) k -> p (j k)", j=BLOCKS),
            )

        load_rows("x", 0)
        load_rows("sp", 0)
        for u in range(2):
            load_weights("d", u)
            load_weights("r", u)
        load_rows("m", 0)
        for c in range(1, CHUNKS):
            for a in ("x", "sp", "m"):
                load_rows(a, c)

        ident = keep.tile([P, P], F32, name="ident")
        make_identity(nc, ident[:])
        scr = ps_scr.tile([P, D], F32, name="scr")

        def keep_clock():
            nc.tensor.matmul(out=scr[:, 0:P], lhsT=ident[:], rhs=ident[:], start=True, stop=True)

        warm = keep.tile([P, 1], F32, name="warm")
        warm2 = keep.tile([P, 1], F32, name="warm2")
        nc.vector.memset(warm[:], 0.0)
        nc.scalar.activation(out=warm2[:], in_=warm[:], func=ACT.Exp)

        rtau = keep.tile([P, TILES], F32, name="rtau")
        alpha = keep.tile([P, TILES], F32, name="alpha")
        gain = keep.tile([P, TILES], F32, name="gain")
        bsum = keep.tile([P, TILES], F32, name="bsum")
        cbias = keep.tile([P, TILES], F32, name="cbias")
        nc.vector.reciprocal(out=rtau[:], in_=tau_bf[:])
        nc.scalar.activation(out=alpha[:], in_=rtau[:], func=ACT.Exp, scale=-1.0)
        nc.vector.tensor_tensor(out=bsum[:], in0=bd_bf[:], in1=br_bf[:], op=ALU.add)
        nc.vector.tensor_scalar(
            out=gain[:], in0=alpha[:], scalar1=-1.0, scalar2=1.0, op0=ALU.mult, op1=ALU.add
        )
        nc.vector.tensor_tensor(out=cbias[:], in0=bsum[:], in1=gain[:], op=ALU.mult)

        def mx_operand(name, cols):
            grouped = keep.tile([P, cols * 4], BF16, name="g_%s" % name, align_bytes=64)
            codes = keep.tile([P, cols], U32, name="c_%s" % name, align_bytes=64)
            scales = keep.tile([P, cols], U8, name="s_%s" % name, align_bytes=64)
            return grouped, codes, scales

        w_mx = {}
        for w in ("d", "r"):
            w_mx[w] = mx_operand("w%s" % w, D)
        a_mx = {}
        for c in range(CHUNKS):
            for a in ("x", "sp"):
                a_mx[(a, c)] = mx_operand("%s%d" % (a, c), ROWS)
        o_sb = {}
        for c in range(CHUNKS):
            for which in range(2):
                o_sb[(c, which)] = keep.tile([P, BLOCKS * D], F32, name="o%d_%d" % (which, c))
        bank = {}
        z_sb = {}
        y_sb = {}

        def transpose_words(src, first, name):
            t = ps_tp.tile([P, D], F32, name=name, tag="tp")
            words = src[:].bitcast(F32)
            for b in range(2):
                for h in range(2):
                    nc.tensor.transpose(
                        t[:, h * GROUP + b * P : h * GROUP + (b + 1) * P],
                        words[:, (first + b) * WORDS + h * P : (first + b) * WORDS + (h + 1) * P],
                        ident[:],
                    )
            return t

        def copy_words(engine, t, grouped, first):
            dst = grouped[:].bitcast(F32)[:, first * WORDS : (first + 2) * WORDS].rearrange("p (n h) -> p n h", h=2)
            src = t[:, 0 : 2 * GROUP].rearrange("p (h n) -> p n h", h=2)
            if engine == "scalar":
                nc.scalar.copy(out=dst, in_=src)
            else:
                nc.vector.tensor_copy(out=dst, in_=src)

        def quantise(operand, c0, c1):
            grouped, codes, scales = operand
            nc.vector.quantize_mx(
                out=codes[:, c0:c1].bitcast(FP8X4), scales=scales[:, c0:c1], in_=grouped[:, 4 * c0 : 4 * c1]
            )

        def transpose_weights(w, u):
            bank[(w, u)] = transpose_words(w_sb[w], 2 * u, "tp_w%s%d" % (w, u))

        def copy_weights(w, u, engine):
            copy_words(engine, bank[(w, u)], w_mx[w][0], 2 * u)

        def quantise_weights(w, u):
            quantise(w_mx[w], u * GROUP, (u + 1) * GROUP)

        def transpose_rows(a, c):
            bank[(a, c)] = transpose_words(a_sb[(a, c)], 0, "tp_%s%d_0" % (a, c))

        def copy_rows(a, c, engine):
            copy_words(engine, bank[(a, c)], a_mx[(a, c)][0], 0)

        def quantise_rows(a, c):
            quantise(a_mx[(a, c)], 0, ROWS)

        def transpose_mem(c):
            t = ps_tp.tile([P, D], F32, name="tm_%d" % c, tag="tp")
            words = a_sb[("m", c)][:].bitcast(F32)
            for u in range(2):
                for j in range(BLOCKS):
                    nc.tensor.transpose(
                        t[:, u * ROWS + j * P : u * ROWS + (j + 1) * P],
                        words[:, j * WORDS + u * P : j * WORDS + (u + 1) * P],
                        ident[:],
                    )
            bank[("m", c)] = t

        def decay_mem(c):
            for t in range(TILES):
                u, e = divmod(t, 2)
                z_sb[(c, t)] = keep.tile([P, ROWS], F32, name="z_%d_%d" % (c, t))
                nc.scalar.activation(
                    out=z_sb[(c, t)][:],
                    in_=bank[("m", c)][:, u * ROWS : (u + 1) * ROWS]
                    .bitcast(BF16)
                    .rearrange("p (n e) -> p n e", e=2)[:, :, e],
                    func=ACT.Identity,
                    bias=cbias[:, t : t + 1],
                    scale=alpha[:, t : t + 1],
                )

        def matmuls(c, tiles):
            for t in tiles:
                if t % 2 == 0:
                    bank[("pair", c)] = ps_acc.tile([P, D], F32, name="acc_%d_%d" % (c, t), tag="acc")
                acc = bank[("pair", c)][:, (t % 2) * ROWS : (t % 2 + 1) * ROWS]
                bank[("acc", c, t)] = acc
                cols = slice(t * P, (t + 1) * P)
                for first, w, a in ((True, "d", "x"), (False, "r", "sp")):
                    nc.tensor.matmul_mx(
                        out=acc,
                        lhsT=w_mx[w][1][:, cols].bitcast(FP8X4),
                        lhsT_scale=w_mx[w][2][:, cols],
                        rhs=a_mx[(a, c)][1][:].bitcast(FP8X4),
                        rhs_scale=a_mx[(a, c)][2][:],
                        start=first,
                        stop=not first,
                    )

        def update(c):
            for t in range(TILES):
                y_sb[(c, t)] = keep.tile([P, ROWS], F32, name="y_%d_%d" % (c, t))
                nc.vector.scalar_tensor_tensor(
                    out=y_sb[(c, t)][:],
                    in0=bank[("acc", c, t)],
                    scalar=gain[:, t : t + 1],
                    in1=z_sb[(c, t)][:],
                    op0=ALU.mult,
                    op1=ALU.add,
                )

        def transpose_back(c, j):
            ty = ps_ty.tile([P, D], F32, name="ty_%d_%d" % (c, j), tag="ty")
            for t in range(TILES):
                u, e = divmod(t, 2)
                nc.tensor.transpose(
                    ty[:, e * WORDS + u * P : e * WORDS + (u + 1) * P], y_sb[(c, t)][:, j * P : (j + 1) * P], ident[:]
                )
            bank[("ty", c, j)] = ty

        def reset(c, j):
            cols = slice(j * D, (j + 1) * D)
            nc.vector.scalar_tensor_tensor(
                out=o_sb[(c, 0)][:, cols].rearrange("p (w e) -> p w e", e=2),
                in0=a_sb[("sp", c)][:, cols].rearrange("p (w e) -> p w e", e=2),
                scalar=-THRESH,
                in1=bank[("ty", c, j)][:].rearrange("p (e w) -> p w e", e=2),
                op0=ALU.mult,
                op1=ALU.add,
            )

        def fire(c, j, engine):
            cols = slice(j * D, (j + 1) * D)
            v = o_sb[(c, 0)][:, cols]
            s = o_sb[(c, 1)][:, cols]
            if engine == "vector":
                nc.vector.tensor_single_scalar(out=s, in_=v, scalar=THRESH, op=ALU.is_gt)
            else:
                nc.gpsimd.tensor_scalar(out=s, in0=v, scalar1=-THRESH, scalar2=STEEP, op0=ALU.add, op1=ALU.mult)
                nc.gpsimd.tensor_scalar(out=s, in0=s, scalar1=1.0, scalar2=0.0, op0=ALU.min, op1=ALU.max)

        def store(c, which, j0, j1):
            cols = slice(j0 * D, j1 * D)
            dram = out_0 if which == 0 else out_1
            nc.sync.dma_start(
                out=dram[c * ROWS : (c + 1) * ROWS, :].rearrange("(p j) o -> p (j o)", j=BLOCKS)[:, cols],
                in_=o_sb[(c, which)][:, cols],
            )

        for keeper in range(4):
            keep_clock()
        transpose_rows("x", 0)
        copy_rows("x", 0, "scalar")
        transpose_rows("sp", 0)
        keep_clock()
        keep_clock()
        copy_rows("sp", 0, "vector")
        quantise_rows("x", 0)
        quantise_rows("sp", 0)
        transpose_weights("d", 0)
        copy_weights("d", 0, "scalar")
        quantise_weights("d", 0)
        transpose_weights("r", 0)
        keep_clock()
        keep_clock()
        copy_weights("r", 0, "scalar")
        transpose_weights("d", 1)
        copy_weights("d", 1, "vector")
        quantise_weights("r", 0)
        quantise_weights("d", 1)
        transpose_weights("r", 1)
        keep_clock()
        keep_clock()
        copy_weights("r", 1, "scalar")
        quantise_weights("r", 1)
        transpose_mem(0)
        decay_mem(0)
        matmuls(0, (0, 1))
        transpose_rows("x", 1)
        matmuls(0, (2, 3))

        for c in range(CHUNKS):
            if c > 0:
                matmuls(c, (0, 1, 2, 3))
            if c + 1 < CHUNKS:
                copy_rows("x", c + 1, "scalar")
                transpose_rows("sp", c + 1)
                transpose_mem(c + 1)
            if c + 2 < CHUNKS:
                transpose_rows("x", c + 2)
            if c + 1 < CHUNKS:
                copy_rows("sp", c + 1, "scalar")
                decay_mem(c + 1)
            update(c)
            if c > 0:
                fire(c - 1, 1, "vector")
                store(c - 1, 1, 0, BLOCKS)
            if c + 1 < CHUNKS:
                quantise_rows("x", c + 1)
                quantise_rows("sp", c + 1)
            for j in range(BLOCKS):
                transpose_back(c, j)
            if c + 1 < CHUNKS:
                reset(c, 0)
                fire(c, 0, "gpsimd")
                reset(c, 1)
                store(c, 0, 0, BLOCKS)

        last = CHUNKS - 1
        for j in range(BLOCKS):
            reset(last, j)
            store(last, 0, j, j + 1)
            fire(last, j, "vector")
            store(last, 1, j, j + 1)
